import numpy as np
import ml_dtypes


def mxq(x, axis, fmt="e4m3"):
    dtype, down = {"e4m3": (ml_dtypes.float8_e4m3fn, 7), "e5m2": (ml_dtypes.float8_e5m2, 14)}[fmt]
    v = np.moveaxis(np.asarray(x, np.float32).astype(ml_dtypes.bfloat16).astype(np.float64), axis, -1)
    blocks = v.reshape(v.shape[:-1] + (-1, 32))
    amax = np.abs(blocks).max(-1, keepdims=True)
    byte = np.maximum(np.where(amax > 0, np.frexp(amax)[1] - 1 + 127, 0) - down, 1)
    scale = np.exp2(byte - 127.0)
    codes = (blocks / scale).astype(np.float32).astype(dtype).astype(np.float64)
    return np.moveaxis((codes * scale).reshape(v.shape), -1, axis)


WIDE = False


def mx_kscale(k):
    if not WIDE:
        return np.ones(k)
    levels = np.array([10, -10, 5, -5, 0])
    if k % 512:
        return np.exp2(np.random.permutation(np.resize(levels, k // 32))).repeat(32)
    a = np.empty((k // 512, 16))
    for p in range(k // 512):
        a[p, :8] = np.random.permutation(np.resize(levels, 8))
        for g in range(8):
            far = levels[np.abs(levels - a[p, g]) >= 10]
            a[p, g + 8] = far[np.random.randint(len(far))]
    return np.exp2(a.ravel()).repeat(32)


BF16 = ml_dtypes.bfloat16


def bf(x):
    return np.asarray(x, np.float32).astype(BF16)


def f64(x):
    return np.asarray(x).astype(np.float64)


B, S, HID, NH, NKV, LORA, D_ROPE, D_NOPE, D_V = 2, 256, 2048, 16, 4, 512, 64, 128, 128
D_QK = D_NOPE + D_ROPE
ROPE_BASE = 10000.0


def rope(x):
    inv_freq = 1.0 / (ROPE_BASE ** (f64(np.arange(0, D_ROPE, 2)) / D_ROPE))
    freqs = np.outer(f64(np.arange(S)), inv_freq)
    emb = np.concatenate([freqs, freqs], axis=-1)
    cos = np.cos(emb)[None, :, None, :]
    sin = np.sin(emb)[None, :, None, :]
    x1, x2 = np.split(x, 2, axis=-1)
    rot = np.concatenate([-x2, x1], axis=-1)
    return x * cos + rot * sin


def draw0():
    s, t = mx_kscale(HID), mx_kscale(LORA)
    col = np.concatenate([np.ones(NH * D_QK), t])
    return {
        "hidden_states": bf(np.random.standard_normal((B, S, HID)) * s),
        "Wqkv": bf(np.random.standard_normal((HID, NH * D_QK + LORA)) / np.sqrt(HID) / s[:, None] * col),
        "Wk_up": bf(np.random.standard_normal((LORA, NKV * D_QK)) / np.sqrt(LORA) / t[:, None]),
        "Wv_up": bf(np.random.standard_normal((LORA, NKV * D_V)) / np.sqrt(LORA) / t[:, None]),
    }


def core(hidden_states, Wqkv, Wk_up, Wv_up):
    qkv = mxq(f64(hidden_states), 2, "e4m3") @ mxq(f64(Wqkv), 0, "e4m3")
    q, c_kv = np.split(qkv, [NH * D_QK], axis=-1)
    q = q.reshape(B, S, NH, D_QK)
    cq = mxq(c_kv, 2, "e4m3")
    k = (cq @ mxq(f64(Wk_up), 0, "e4m3")).reshape(B, S, NKV, D_QK)
    v = (cq @ mxq(f64(Wv_up), 0, "e4m3")).reshape(B, S, NKV, D_V)
    q_nope, q_rope = np.split(q, [D_NOPE], axis=-1)
    k_nope, k_rope = np.split(k, [D_NOPE], axis=-1)
    q = np.concatenate([q_nope, rope(q_rope)], axis=-1)
    k = np.concatenate([k_nope, rope(k_rope)], axis=-1)
    return q, k, v


def e4m3fn_bytes(y):
    return np.clip(np.asarray(y, np.float64), -448.0, 448.0).astype(np.float32).astype(ml_dtypes.float8_e4m3fn).view(np.uint8)


def e4m3fn_values(b):
    return np.asarray(b, np.uint8).view(ml_dtypes.float8_e4m3fn).astype(np.float64)


def setup_inputs():
    d = draw0()
    x0 = np.asarray(d['hidden_states']).astype(np.float64)
    s = (np.max(np.abs(x0), axis=(0, 1), keepdims=True) / 448.0).astype(np.float32)
    out = {}
    for k, v in d.items():
        if k == 'hidden_states':
            out['hidden_states_bytes'] = e4m3fn_bytes(x0 / s.astype(np.float64))
            out['hidden_states_scale'] = s
        else:
            out[k] = v
    return out


def reference(hidden_states_bytes, hidden_states_scale, Wqkv, Wk_up, Wv_up):
    return core(e4m3fn_values(hidden_states_bytes) * hidden_states_scale.astype(np.float64), Wqkv, Wk_up, Wv_up)

@@ -1,0 +1,405 @@
+import math
+from contextlib import ExitStack
+
+import concourse.mybir as mybir
+from concourse.masks import make_identity
+
+F32 = mybir.dt.float32
+BF16 = mybir.dt.bfloat16
+U32 = mybir.dt.uint32
+I32 = mybir.dt.int32
+U8 = mybir.dt.uint8
+E4M3 = mybir.dt.float8_e4m3fn
+X4 = mybir.dt.float8_e4m3fn_x4
+ALU = mybir.AluOpType
+ACT = mybir.ActivationFunctionType
+
+B, S, HID, NH, NKV, LORA, D_ROPE, D_NOPE, D_V = 2, 256, 2048, 16, 4, 512, 64, 128, 128
+D_QK = D_NOPE + D_ROPE
+P = 128
+FLOPS = 2 * B * S * (HID * (NH * D_QK + LORA) + LORA * NKV * (D_QK + D_V))
+
+MB = B * S // P
+KP = HID // 512
+GH = 4
+GW = GH * D_QK
+GN = GH * D_NOPE
+GR = GH * D_ROPE
+NG = NH // GH
+HALF = D_ROPE // 2
+ROW_BUFS = 10
+LOOK = 9
+
+VECTOR_A = {(1, 1), (2, 1), (3, 1), (3, 3)}
+
+
+def tile_multiheadlatentattentionwithgqafused_pa_kernel(
+    tc, x_bytes, x_scale, wqkv, wk_up, wv_up, q_out, k_out, v_out
+):
+    nc = tc.nc
+    with ExitStack() as ctx:
+        one = ctx.enter_context(tc.tile_pool(name="one", bufs=1))
+        rows = ctx.enter_context(tc.tile_pool(name="rows", bufs=ROW_BUFS))
+        xpool = ctx.enter_context(tc.tile_pool(name="xpool", bufs=2))
+        grp = ctx.enter_context(tc.tile_pool(name="grp", bufs=3))
+        codes = ctx.enter_context(tc.tile_pool(name="codes", bufs=12))
+        outs = ctx.enter_context(tc.tile_pool(name="outs", bufs=3))
+        tmp = ctx.enter_context(tc.tile_pool(name="tmp", bufs=2))
+        psum = ctx.enter_context(tc.psum_pool(name="psum", bufs=1))
+
+        def bank(tag, bufs):
+            acc = psum.tile([P, 512], F32, name=tag, tag=tag, bufs=bufs)
+            return acc
+
+        sc = one.tile([P, KP, 2, 2], F32, name="sc")
+        nc.sync.dma_start(
+            out=sc[:].rearrange("p g u e -> p g (u e)"),
+            in_=x_scale.rearrange("a b (g p t) -> p (a b g) t", p=P, t=4),
+        )
+        xby = []
+        for m in range(MB):
+            xb8 = one.tile([P, HID], U8, name="xb8_%d" % m)
+            nc.sync.dma_start(out=xb8[:], in_=x_bytes[m // 2, (m % 2) * P : (m % 2 + 1) * P, :])
+            xby.append(xb8)
+
+        wq = wqkv.rearrange("(g p j) n -> g p j n", p=P, j=4)
+        chunks = [("L", g) for g in range(KP)] + [(0, g) for g in range(KP)] + [("K", 0), ("V", 0)]
+        chunks += [(G, g) for G in range(1, NG) for g in range(KP)]
+        raw = {}
+
+        def load(i):
+            if i >= len(chunks):
+                return
+            kind, g = chunks[i]
+            if kind == "L":
+                src = wq[g][:, :, NH * D_QK :]
+            elif kind == "K":
+                src = wk_up.rearrange("(p j) n -> p j n", j=4)
+            elif kind == "V":
+                src = wv_up.rearrange("(p j) n -> p j n", j=4)
+            else:
+                src = wq[g][:, :, kind * GW : (kind + 1) * GW]
+            w = src.shape[2]
+            r = rows.tile([P, 4, GW], BF16, name="raw", tag="raw", align_bytes=64)
+            flat = r[:].rearrange("p j w -> p (j w)")[:, : 4 * w].rearrange("p (j w) -> p j w", j=4)
+            nc.sync.dma_start(out=flat, in_=src)
+            raw[chunks[i]] = flat
+
+        for i in range(LOOK):
+            load(i)
+
+        ident = one.tile([P, P], F32, name="ident")
+        make_identity(nc, ident[:])
+        pos = one.tile([P, 2], F32, name="pos")
+        nc.gpsimd.iota(
+            pos[:], pattern=[[P, 2]], base=0, channel_multiplier=1, allow_small_or_imprecise_dtypes=True
+        )
+        ang = one.tile([P, 2, 2, HALF], F32, name="ang")
+        ratio = 10000.0 ** (-1.0 / HALF)
+        nc.vector.tensor_scalar(
+            out=ang[:, 0, :, 0:1], in0=pos[:].rearrange("p (m o) -> p m o", o=1), scalar1=1.0, scalar2=None, op0=ALU.mult
+        )
+        w = 1
+        while w < HALF:
+            nc.vector.tensor_scalar(
+                out=ang[:, 0, :, w : 2 * w], in0=ang[:, 0, :, 0:w], scalar1=ratio**w, scalar2=None, op0=ALU.mult
+            )
+            w *= 2
+        nc.vector.tensor_scalar(
+            out=ang[:, 1], in0=ang[:, 0], scalar1=math.pi / 2, scalar2=None, op0=ALU.add
+        )
+        turn = one.tile([P, 2, 2, HALF], F32, name="turn")
+        turn_i = one.tile([P, 2, 2, HALF], I32, name="turn_i")
+        nc.vector.tensor_scalar(out=turn[:], in0=ang[:], scalar1=1.0 / (2 * math.pi), scalar2=None, op0=ALU.mult)
+        nc.vector.tensor_copy(out=turn_i[:], in_=turn[:])
+        nc.vector.tensor_copy(out=turn[:], in_=turn_i[:])
+        c1 = 6.28125
+        red = one.tile([P, 2, 2, HALF], F32, name="red")
+        flat4 = "p a b c -> p (a b c)"
+        nc.vector.scalar_tensor_tensor(
+            out=red[:].rearrange(flat4), in0=turn[:].rearrange(flat4), scalar=-c1, in1=ang[:].rearrange(flat4),
+            op0=ALU.mult, op1=ALU.add,
+        )
+        red2 = one.tile([P, 2, 2, HALF], F32, name="red2")
+        nc.vector.scalar_tensor_tensor(
+            out=red2[:].rearrange(flat4), in0=turn[:].rearrange(flat4), scalar=c1 - 2 * math.pi, in1=red[:].rearrange(flat4),
+            op0=ALU.mult, op1=ALU.add,
+        )
+        cs1 = one.tile([P, 2, D_ROPE], F32, name="cs1")
+        sn1 = one.tile([P, 2, D_ROPE], F32, name="sn1")
+        nc.scalar.activation(out=cs1[:, :, :HALF], in_=red2[:, 1], func=ACT.Sin)
+        nc.scalar.activation(out=cs1[:, :, HALF:], in_=red2[:, 1], func=ACT.Sin)
+        nc.scalar.activation(out=sn1[:, :, :HALF], in_=red2[:, 0], func=ACT.Sin, scale=-1.0)
+        nc.scalar.activation(out=sn1[:, :, HALF:], in_=red2[:, 0], func=ACT.Sin)
+        cs = one.tile([P, 2, GH, D_ROPE], F32, name="cs")
+        sn = one.tile([P, 2, GH, D_ROPE], F32, name="sn")
+        for h in range(GH):
+            nc.gpsimd.tensor_scalar(out=cs[:, :, h], in0=cs1[:], scalar1=1.0, scalar2=0.0, op0=ALU.mult, op1=ALU.add)
+            nc.gpsimd.tensor_scalar(out=sn[:, :, h], in0=sn1[:], scalar1=1.0, scalar2=0.0, op0=ALU.mult, op1=ALU.add)
+
+        xcast, xgrp, xcode = {}, {}, {}
+
+        def cast_x(m):
+            xb = xpool.tile([P, HID], BF16, name="xb", tag="xb", align_bytes=64)
+            if m % 2 == 0:
+                nc.vector.tensor_copy(out=xb[:], in_=xby[m][:].bitcast(E4M3))
+            else:
+                nc.scalar.copy(out=xb[:], in_=xby[m][:].bitcast(E4M3))
+            xcast[m] = xb
+
+        def turn_x(m):
+            words = xcast[m][:].bitcast(F32)
+            xg = xpool.tile([P, KP, P, 2, 2], BF16, name="xg", tag="xg", align_bytes=64)
+            for half in range(2):
+                xt = bank("np", 4)
+                for gg in range(2):
+                    for u in range(2):
+                        g = 2 * half + gg
+                        nc.tensor.transpose(
+                            xt[:, (2 * gg + u) * P : (2 * gg + u + 1) * P],
+                            words[:, 256 * g + u : 256 * (g + 1) : 2],
+                            ident[:],
+                        )
+                halves = xt[:].bitcast(BF16).rearrange("p (g u r e) -> p g r u e", g=2, u=2, e=2)
+                for gg in range(2):
+                    g = 2 * half + gg
+                    nc.vector.tensor_tensor(
+                        out=xg[:, g], in0=halves[:, gg], in1=sc[:, g : g + 1].to_broadcast([P, P, 2, 2]), op=ALU.mult
+                    )
+            xgrp[m] = xg
+
+        def quant_x(m):
+            xc = one.tile([P, KP, P], U32, name="xc_%d" % m, align_bytes=64)
+            xs = one.tile([P, KP, P], U8, name="xs_%d" % m, align_bytes=64)
+            nc.vector.quantize_mx(
+                out=xc[:].rearrange("p g r -> p (g r)").bitcast(X4),
+                scales=xs[:].rearrange("p g r -> p (g r)"),
+                in_=xgrp[m][:].rearrange("p g r u e -> p (g r u e)"),
+            )
+            xcode[m] = (xc, xs)
+
+        grouped, wcode = {}, {}
+
+        def interleave(i):
+            key = chunks[i]
+            kind, g = key
+            src = raw[key]
+            ga = grp.tile([P, 2048], BF16, name="ga", tag="ga", align_bytes=64)
+            if kind == "L":
+                nc.gpsimd.tensor_scalar(
+                    out=ga[:].rearrange("p (t m j) -> p t m j", t=4, j=4),
+                    in0=src.rearrange("p j (m t) -> p t m j", t=4),
+                    scalar1=1.0, scalar2=0.0, op0=ALU.mult, op1=ALU.add,
+                )
+                grouped[key] = (ga, None)
+                return
+            if kind == "V":
+                nc.scalar.copy(
+                    out=ga[:].rearrange("p (c i j) -> p c j i", i=4, j=4),
+                    in_=src.rearrange("p j (c i) -> p c j i", i=4),
+                )
+                grouped[key] = (ga, None)
+                return
+            heads = src.rearrange("p j (h d) -> p j h d", d=D_QK)
+            da = ga[:].rearrange("p (h c i j) -> p h c j i", h=GH, i=4, j=4)
+            sa = heads[:, :, :, :D_NOPE].rearrange("p j h (c i) -> p h c j i", i=4)
+            if key in VECTOR_A:
+                nc.vector.tensor_copy(out=da, in_=sa)
+            else:
+                nc.scalar.copy(out=da, in_=sa)
+            gb = grp.tile([P, 1024], BF16, name="gb", tag="gb", align_bytes=64)
+            nc.vector.tensor_copy(
+                out=gb[:].rearrange("p (h c i j) -> p h c j i", h=GH, i=4, j=4),
+                in_=heads[:, :, :, D_NOPE:].rearrange("p j h (c i) -> p h c j i", i=4),
+            )
+            grouped[key] = (ga, gb)
+
+        def quant(i):
+            key = chunks[i]
+            kind = key[0]
+            ga, gb = grouped[key]
+            if kind in ("L", "K", "V"):
+                wc = one.tile([P, GW], U32, name="wc_%s%d" % key, align_bytes=64)
+                ws = one.tile([P, GW], U8, name="ws_%s%d" % key, align_bytes=64)
+            else:
+                wc = codes.tile([P, GW], U32, name="wc", tag="wc", align_bytes=64)
+                ws = codes.tile([P, GW], U8, name="ws", tag="ws", align_bytes=64)
+            nc.vector.quantize_mx(out=wc[:, :512].bitcast(X4), scales=ws[:, :512], in_=ga[:])
+            if gb is not None:
+                nc.vector.quantize_mx(out=wc[:, 512:].bitcast(X4), scales=ws[:, 512:], in_=gb[:])
+            wcode[key] = (wc, ws)
+
+        def mm(out, left, lcols, right, rcols, start, stop):
+            nc.tensor.matmul_mx(
+                out=out,
+                lhsT=left[0][:, lcols].bitcast(X4), lhsT_scale=left[1][:, lcols],
+                rhs=right[0][:, rcols].bitcast(X4), rhs_scale=right[1][:, rcols],
+                start=start, stop=stop,
+            )
+
+        def xflat(m):
+            return tuple(t[:].rearrange("p g r -> p (g r)") for t in xcode[m])
+
+        ckg = one.tile([P, MB, P, 4], BF16, name="ckg", align_bytes=64)
+        ckc = one.tile([P, MB * P], U32, name="ckc", align_bytes=64)
+        cks = one.tile([P, MB * P], U8, name="cks", align_bytes=64)
+        ckb = {}
+
+        def mm_latent(m):
+            acc = bank("mx", 2)
+            for t in range(4):
+                for g in range(KP):
+                    mm(
+                        acc[:, t * P : (t + 1) * P], wcode[("L", g)], slice(t * P, (t + 1) * P),
+                        xflat(m), slice(g * P, (g + 1) * P), g == 0, g == KP - 1,
+                    )
+            ckb[m] = acc
+
+        def evac_latent(m):
+            nc.scalar.copy(out=ckg[:, m], in_=ckb[m][:].rearrange("p (t n) -> p n t", t=4))
+
+        def quant_latent(b):
+            nc.vector.quantize_mx(
+                out=ckc[:, 2 * b * P : 2 * (b + 1) * P].bitcast(X4),
+                scales=cks[:, 2 * b * P : 2 * (b + 1) * P],
+                in_=ckg[:, 2 * b : 2 * b + 2].rearrange("p m n t -> p (m n t)"),
+            )
+
+        banks = {}
+
+        def mm_group(kind, b):
+            nope = []
+            rope = bank("rp", 2) if kind != "V" else None
+            for mi in range(2):
+                m = 2 * b + mi
+                acc = bank("np", 4)
+                if kind in ("K", "V"):
+                    mm(acc[:], (ckc, cks), slice(m * P, (m + 1) * P), wcode[(kind, 0)], slice(0, GN), True, True)
+                    if kind == "K":
+                        mm(rope[:, mi * GR : (mi + 1) * GR], (ckc, cks), slice(m * P, (m + 1) * P),
+                           wcode[(kind, 0)], slice(GN, GW), True, True)
+                else:
+                    for g in range(KP):
+                        mm(acc[:], xflat(m), slice(g * P, (g + 1) * P), wcode[(kind, g)], slice(0, GN), g == 0, g == KP - 1)
+                    for g in range(KP):
+                        mm(rope[:, mi * GR : (mi + 1) * GR], xflat(m), slice(g * P, (g + 1) * P),
+                           wcode[(kind, g)], slice(GN, GW), g == 0, g == KP - 1)
+                nope.append(acc)
+            banks[(kind, b)] = (nope, rope)
+
+        def rotate(rope, cos, sin, out):
+            n = rope.shape[1]
+            a = tmp.tile([P, 512], F32, name="ra", tag="ra")
+            c = tmp.tile([P, 512], F32, name="rc", tag="rc")
+            nc.vector.tensor_tensor(out=a[:, :n], in0=rope, in1=cos, op=ALU.mult)
+            four = "p (a s j) -> p a s j"
+            nc.vector.tensor_tensor(
+                out=c[:, :n].rearrange(four, s=2, j=HALF),
+                in0=rope.rearrange(four, s=2, j=HALF)[:, :, ::-1, :],
+                in1=sin.rearrange(four, s=2, j=HALF),
+                op=ALU.mult,
+            )
+            nc.vector.tensor_tensor(
+                out=out,
+                in0=a[:, :n].rearrange("p (a d) -> p a d", d=D_ROPE),
+                in1=c[:, :n].rearrange("p (a d) -> p a d", d=D_ROPE),
+                op=ALU.add,
+            )
+
+        csf = cs[:].rearrange("p m h d -> p (m h d)")
+        snf = sn[:].rearrange("p m h d -> p (m h d)")
+
+        def evac(kind, b):
+            nope, rope = banks[(kind, b)]
+            if kind == "V":
+                ot = outs.tile([P, 2, GN], F32, name="ov", tag="ov", bufs=2)
+                for mi in range(2):
+                    nc.scalar.copy(out=ot[:, mi], in_=nope[mi][:])
+                nc.sync.dma_start(out=v_out[b].rearrange("(m p) h d -> p m (h d)", p=P), in_=ot[:])
+                return
+            ot = outs.tile([P, 2, GH, D_QK], F32, name="ot", tag="ot")
+            for mi in range(2):
+                nc.scalar.copy(out=ot[:, mi, :, :D_NOPE], in_=nope[mi][:].rearrange("p (h d) -> p h d", h=GH))
+            rotate(rope[:], csf, snf, ot[:].rearrange("p m h d -> p (m h) d")[:, :, D_NOPE:])
+            if kind == "K":
+                dst = k_out[b].rearrange("(m p) h d -> p m (h d)", p=P)
+            else:
+                dst = q_out[b].rearrange("(m p) h d -> p m (h d)", p=P)[:, :, kind * GW : (kind + 1) * GW]
+            nc.sync.dma_start(out=dst, in_=ot[:].rearrange("p m h d -> p m (h d)"))
+
+        last = {}
+
+        def last_pass(m, g):
+            if g == 0:
+                last[m] = (bank("np", 4), bank("rp" if m % 2 == 0 else "mx", 2))
+            nope, rope = last[m]
+            xm = xflat(m)
+            mm(nope[:], xm, slice(g * P, (g + 1) * P), wcode[(NG - 1, g)], slice(0, GN), g == 0, g == KP - 1)
+            mm(rope[:, :GR], xm, slice(g * P, (g + 1) * P), wcode[(NG - 1, g)], slice(GN, GW), g == 0, g == KP - 1)
+
+        def last_evac(m):
+            nope, rope = last[m]
+            ot = outs.tile([P, 2, GH, D_QK], F32, name="ot", tag="ot")
+            nc.scalar.copy(out=ot[:, 0, :, :D_NOPE], in_=nope[:].rearrange("p (h d) -> p h d", h=GH))
+            mi = m % 2
+            rotate(rope[:, :GR], csf[:, mi * GR : (mi + 1) * GR], snf[:, mi * GR : (mi + 1) * GR], ot[:, 0, :, D_NOPE:])
+            nc.sync.dma_start(
+                out=q_out[m // 2, mi * P : (mi + 1) * P].rearrange("s h d -> s (h d)")[:, (NG - 1) * GW :],
+                in_=ot[:, 0].rearrange("p h d -> p (h d)"),
+            )
+
+        cast_x(0)
+        cast_x(1)
+        turn_x(0)
+        interleave(0)
+        cast_x(2)
+        turn_x(1)
+        quant_x(0)
+        interleave(1)
+        cast_x(3)
+        quant(0)
+        turn_x(2)
+        quant_x(1)
+        interleave(2)
+        quant(1)
+        turn_x(3)
+        quant_x(2)
+        interleave(3)
+        quant(2)
+        quant_x(3)
+        for i in range(4):
+            load(LOOK + i)
+
+        after = {}
+        idx = {key: i for i, key in enumerate(chunks)}
+        after[idx[(0, 1)]] = [lambda: mm_latent(0), lambda: mm_latent(1)]
+        after[idx[(0, 2)]] = [
+            lambda: evac_latent(0), lambda: evac_latent(1), lambda: mm_latent(2), lambda: mm_latent(3), lambda: quant_latent(0)
+        ]
+        after[idx[(0, 3)]] = [lambda: evac_latent(2), lambda: evac_latent(3)]
+        after[idx[("K", 0)]] = [lambda: quant_latent(1), lambda: mm_group(0, 0), lambda: mm_group(0, 1)]
+        after[idx[("V", 0)]] = [lambda: evac(0, 0)]
+        after[idx[(1, 0)]] = [lambda: evac(0, 1), lambda: mm_group("K", 0), lambda: mm_group("K", 1)]
+        after[idx[(1, 1)]] = [lambda: evac("K", 0), lambda: evac("K", 1)]
+        after[idx[(1, 2)]] = [lambda: mm_group("V", 0), lambda: mm_group("V", 1), lambda: evac("V", 0)]
+        after[idx[(1, 3)]] = [lambda: evac("V", 1)]
+        after[idx[(2, 0)]] = [lambda: mm_group(1, 0), lambda: mm_group(1, 1)]
+        after[idx[(2, 1)]] = [lambda: evac(1, 0)]
+        after[idx[(2, 2)]] = [lambda: evac(1, 1)]
+        after[idx[(3, 0)]] = [lambda: mm_group(2, 0), lambda: mm_group(2, 1)]
+        after[idx[(3, 1)]] = [lambda: evac(2, 0)]
+        after[idx[(3, 2)]] = [lambda: evac(2, 1)]
+
+        for i in range(4, len(chunks)):
+            load(LOOK + i)
+            interleave(i)
+            quant(i - 1)
+            for f in after.get(i, []):
+                f()
+        for g in range(KP - 1):
+            for m in range(MB):
+                last_pass(m, g)
+        quant(len(chunks) - 1)
+        for m in range(MB):
+            last_pass(m, KP - 1)
+            last_evac(m)

@@ -27,10 +27,8 @@ GN = GH * D_NOPE
 GR = GH * D_ROPE
 NG = NH // GH
 HALF = D_ROPE // 2
-ROW_BUFS = 10
-LOOK = 9
-
-VECTOR_A = {(1, 1), (2, 1), (3, 1), (3, 3)}
+LATENT_SCALAR = (0, 1, 2)
+VECTOR_HEADS = {(0, 0): 4, (2, 0): 4, (0, 3): 2}
 
 
 def tile_multiheadlatentattentionwithgqafused_pa_kernel(
@@ -39,10 +37,10 @@ def tile_multiheadlatentattentionwithgqafused_pa_kernel(
     nc = tc.nc
     with ExitStack() as ctx:
         one = ctx.enter_context(tc.tile_pool(name="one", bufs=1))
-        rows = ctx.enter_context(tc.tile_pool(name="rows", bufs=ROW_BUFS))
+        rows = ctx.enter_context(tc.tile_pool(name="rows", bufs=4))
         xpool = ctx.enter_context(tc.tile_pool(name="xpool", bufs=2))
-        grp = ctx.enter_context(tc.tile_pool(name="grp", bufs=3))
-        codes = ctx.enter_context(tc.tile_pool(name="codes", bufs=12))
+        grp = ctx.enter_context(tc.tile_pool(name="grp", bufs=5))
+        codes = ctx.enter_context(tc.tile_pool(name="codes", bufs=9))
         outs = ctx.enter_context(tc.tile_pool(name="outs", bufs=3))
         tmp = ctx.enter_context(tc.tile_pool(name="tmp", bufs=2))
         psum = ctx.enter_context(tc.psum_pool(name="psum", bufs=1))
@@ -63,37 +61,33 @@ def tile_multiheadlatentattentionwithgqafused_pa_kernel(
             xby.append(xb8)
 
         wq = wqkv.rearrange("(g p j) n -> g p j n", p=P, j=4)
-        chunks = [("L", g) for g in range(KP)] + [(0, g) for g in range(KP)] + [("K", 0), ("V", 0)]
-        chunks += [(G, g) for G in range(1, NG) for g in range(KP)]
         raw = {}
 
-        def load(i):
-            if i >= len(chunks):
-                return
-            kind, g = chunks[i]
-            if kind == "L":
-                src = wq[g][:, :, NH * D_QK :]
-            elif kind == "K":
-                src = wk_up.rearrange("(p j) n -> p j n", j=4)
-            elif kind == "V":
-                src = wv_up.rearrange("(p j) n -> p j n", j=4)
-            else:
-                src = wq[g][:, :, kind * GW : (kind + 1) * GW]
+        def load_small(name, src, tag, bufs):
             w = src.shape[2]
-            r = rows.tile([P, 4, GW], BF16, name="raw", tag="raw", align_bytes=64)
-            flat = r[:].rearrange("p j w -> p (j w)")[:, : 4 * w].rearrange("p (j w) -> p j w", j=4)
-            nc.sync.dma_start(out=flat, in_=src)
-            raw[chunks[i]] = flat
+            r = rows.tile([P, 4, w], BF16, name="raw_" + tag, tag=tag, bufs=bufs, align_bytes=64)
+            nc.sync.dma_start(out=r[:], in_=src)
+            raw[name] = r[:]
 
-        for i in range(LOOK):
-            load(i)
+        def load_pair(h, g):
+            r = rows.tile([P, 4, 2 * GW], BF16, name="raw_q", tag="raw_q", align_bytes=64)
+            nc.sync.dma_start(out=r[:], in_=wq[g][:, :, 2 * h * GW : 2 * (h + 1) * GW])
+            for i in range(2):
+                raw[(2 * h + i, g)] = r[:, :, i * GW : (i + 1) * GW]
 
-        ident = one.tile([P, P], F32, name="ident")
-        make_identity(nc, ident[:])
+        for g in range(KP):
+            load_small(("L", g), wq[g][:, :, NH * D_QK :], "raw_l", 4)
+        load_small(("K", 0), wk_up.rearrange("(p j) n -> p j n", j=4), "raw_k", 1)
+        load_small(("V", 0), wv_up.rearrange("(p j) n -> p j n", j=4), "raw_l", 4)
+        for g in range(KP):
+            load_pair(0, g)
+
         pos = one.tile([P, 2], F32, name="pos")
         nc.gpsimd.iota(
             pos[:], pattern=[[P, 2]], base=0, channel_multiplier=1, allow_small_or_imprecise_dtypes=True
         )
+        ident = one.tile([P, P], F32, name="ident")
+        make_identity(nc, ident[:])
         ang = one.tile([P, 2, 2, HALF], F32, name="ang")
         ratio = 10000.0 ** (-1.0 / HALF)
         nc.vector.tensor_scalar(
@@ -140,8 +134,8 @@ def tile_multiheadlatentattentionwithgqafused_pa_kernel(
         xcast, xgrp, xcode = {}, {}, {}
 
         def cast_x(m):
-            xb = xpool.tile([P, HID], BF16, name="xb", tag="xb", align_bytes=64)
-            if m % 2 == 0:
+            xb = xpool.tile([P, HID], BF16, name="xb", tag="xb", align_bytes=64, bufs=2)
+            if m == 0:
                 nc.vector.tensor_copy(out=xb[:], in_=xby[m][:].bitcast(E4M3))
             else:
                 nc.scalar.copy(out=xb[:], in_=xby[m][:].bitcast(E4M3))
@@ -149,7 +143,8 @@ def tile_multiheadlatentattentionwithgqafused_pa_kernel(
 
         def turn_x(m):
             words = xcast[m][:].bitcast(F32)
-            xg = xpool.tile([P, KP, P, 2, 2], BF16, name="xg", tag="xg", align_bytes=64)
+            xgf = xpool.tile([P, 2048], BF16, name="xgf", tag="xgf", align_bytes=64, bufs=4)
+            xg = xgf[:].rearrange("p (g r u e) -> p g r u e", g=KP, u=2, e=2)
             for half in range(2):
                 xt = bank("np", 4)
                 for gg in range(2):
@@ -166,7 +161,7 @@ def tile_multiheadlatentattentionwithgqafused_pa_kernel(
                     nc.vector.tensor_tensor(
                         out=xg[:, g], in0=halves[:, gg], in1=sc[:, g : g + 1].to_broadcast([P, P, 2, 2]), op=ALU.mult
                     )
-            xgrp[m] = xg
+            xgrp[m] = xgf
 
         def quant_x(m):
             xc = one.tile([P, KP, P], U32, name="xc_%d" % m, align_bytes=64)
@@ -174,53 +169,81 @@ def tile_multiheadlatentattentionwithgqafused_pa_kernel(
             nc.vector.quantize_mx(
                 out=xc[:].rearrange("p g r -> p (g r)").bitcast(X4),
                 scales=xs[:].rearrange("p g r -> p (g r)"),
-                in_=xgrp[m][:].rearrange("p g r u e -> p (g r u e)"),
+                in_=xgrp[m][:],
             )
             xcode[m] = (xc, xs)
 
         grouped, wcode = {}, {}
+        sc_copy, ve_copy = nc.scalar.copy, nc.vector.tensor_copy
 
-        def interleave(i):
-            key = chunks[i]
+        def weave(engine_copy, dst, src):
+            if len(src.shape) == 4:
+                n = src.shape[2]
+                engine_copy(out=dst.rearrange("p (h d j) -> p h d j", h=n, j=4), in_=src.rearrange("p j h d -> p h d j"))
+            else:
+                engine_copy(out=dst.rearrange("p (d j) -> p d j", j=4), in_=src.rearrange("p j d -> p d j"))
+
+        def interleave(key):
             kind, g = key
             src = raw[key]
             ga = grp.tile([P, 2048], BF16, name="ga", tag="ga", align_bytes=64)
             if kind == "L":
-                nc.gpsimd.tensor_scalar(
+                engine_copy = sc_copy if g in LATENT_SCALAR else ve_copy
+                engine_copy(
                     out=ga[:].rearrange("p (t m j) -> p t m j", t=4, j=4),
-                    in0=src.rearrange("p j (m t) -> p t m j", t=4),
-                    scalar1=1.0, scalar2=0.0, op0=ALU.mult, op1=ALU.add,
+                    in_=src.rearrange("p j (m t) -> p t m j", t=4),
                 )
                 grouped[key] = (ga, None)
                 return
             if kind == "V":
-                nc.scalar.copy(
-                    out=ga[:].rearrange("p (c i j) -> p c j i", i=4, j=4),
-                    in_=src.rearrange("p j (c i) -> p c j i", i=4),
-                )
+                weave(sc_copy, ga[:], src)
                 grouped[key] = (ga, None)
                 return
             heads = src.rearrange("p j (h d) -> p j h d", d=D_QK)
-            da = ga[:].rearrange("p (h c i j) -> p h c j i", h=GH, i=4, j=4)
-            sa = heads[:, :, :, :D_NOPE].rearrange("p j h (c i) -> p h c j i", i=4)
-            if key in VECTOR_A:
-                nc.vector.tensor_copy(out=da, in_=sa)
-            else:
-                nc.scalar.copy(out=da, in_=sa)
+            n = GH - VECTOR_HEADS.get(key, 0)
+            if n > 0:
+                weave(sc_copy, ga[:, : n * 512], heads[:, :, :n, :D_NOPE])
+            if n < GH:
+                weave(ve_copy, ga[:, n * 512 :], heads[:, :, n:, :D_NOPE])
             gb = grp.tile([P, 1024], BF16, name="gb", tag="gb", align_bytes=64)
-            nc.vector.tensor_copy(
-                out=gb[:].rearrange("p (h c i j) -> p h c j i", h=GH, i=4, j=4),
-                in_=heads[:, :, :, D_NOPE:].rearrange("p j h (c i) -> p h c j i", i=4),
-            )
+            weave(ve_copy, gb[:], heads[:, :, :, D_NOPE:])
             grouped[key] = (ga, gb)
 
-        def quant(i):
-            key = chunks[i]
+        def last_a(g, half, engine_copy):
+            key = (NG - 1, g)
+            ga = last_tiles[g][0]
+            heads = raw[key].rearrange("p j (h d) -> p j h d", d=D_QK)
+            weave(engine_copy, ga[:, half * 1024 : (half + 1) * 1024], heads[:, :, 2 * half : 2 * half + 2, :D_NOPE])
+
+        def last_b(g):
+            key = (NG - 1, g)
+            heads = raw[key].rearrange("p j (h d) -> p j h d", d=D_QK)
+            ga = grp.tile([P, 2048], BF16, name="ga", tag="ga", align_bytes=64)
+            gb = grp.tile([P, 1024], BF16, name="gb", tag="gb", align_bytes=64)
+            wc = codes.tile([P, GW], U32, name="wc", tag="wc", align_bytes=64)
+            ws = codes.tile([P, GW], U8, name="ws", tag="ws", align_bytes=64)
+            last_tiles[g] = (ga, gb)
+            wcode[key] = (wc, ws)
+            weave(ve_copy, gb[:], heads[:, :, :, D_NOPE:])
+
+        def last_quant(g, part):
+            ga, gb = last_tiles[g]
+            wc, ws = wcode[(NG - 1, g)]
+            cols = slice(part * 256, (part + 1) * 256)
+            nc.vector.quantize_mx(
+                out=wc[:, cols].bitcast(X4), scales=ws[:, cols],
+                in_=gb[:] if part == 2 else ga[:, part * 1024 : (part + 1) * 1024],
+            )
+
+        last_tiles = {}
+
+        def quant(key):
             kind = key[0]
             ga, gb = grouped[key]
             if kind in ("L", "K", "V"):
-                wc = one.tile([P, GW], U32, name="wc_%s%d" % key, align_bytes=64)
-                ws = one.tile([P, GW], U8, name="ws_%s%d" % key, align_bytes=64)
+                width = GW if kind == "K" else 512
+                wc = one.tile([P, width], U32, name="wc_%s%d" % key, align_bytes=64)
+                ws = one.tile([P, width], U8, name="ws_%s%d" % key, align_bytes=64)
             else:
                 wc = codes.tile([P, GW], U32, name="wc", tag="wc", align_bytes=64)
                 ws = codes.tile([P, GW], U8, name="ws", tag="ws", align_bytes=64)
@@ -287,119 +310,224 @@ def tile_multiheadlatentattentionwithgqafused_pa_kernel(
                 nope.append(acc)
             banks[(kind, b)] = (nope, rope)
 
-        def rotate(rope, cos, sin, out):
-            n = rope.shape[1]
+        def rotate(rope, add, out):
             a = tmp.tile([P, 512], F32, name="ra", tag="ra")
             c = tmp.tile([P, 512], F32, name="rc", tag="rc")
-            nc.vector.tensor_tensor(out=a[:, :n], in0=rope, in1=cos, op=ALU.mult)
+            nc.vector.tensor_tensor(out=a[:], in0=rope[:], in1=csf, op=ALU.mult)
             four = "p (a s j) -> p a s j"
             nc.vector.tensor_tensor(
-                out=c[:, :n].rearrange(four, s=2, j=HALF),
-                in0=rope.rearrange(four, s=2, j=HALF)[:, :, ::-1, :],
-                in1=sin.rearrange(four, s=2, j=HALF),
+                out=c[:].rearrange(four, s=2, j=HALF),
+                in0=rope[:].rearrange(four, s=2, j=HALF)[:, :, ::-1, :],
+                in1=snf.rearrange(four, s=2, j=HALF),
                 op=ALU.mult,
             )
-            nc.vector.tensor_tensor(
+            add(
                 out=out,
-                in0=a[:, :n].rearrange("p (a d) -> p a d", d=D_ROPE),
-                in1=c[:, :n].rearrange("p (a d) -> p a d", d=D_ROPE),
+                in0=a[:].rearrange("p (a d) -> p a d", d=D_ROPE),
+                in1=c[:].rearrange("p (a d) -> p a d", d=D_ROPE),
                 op=ALU.add,
             )
 
         csf = cs[:].rearrange("p m h d -> p (m h d)")
         snf = sn[:].rearrange("p m h d -> p (m h d)")
 
-        def evac(kind, b):
-            nope, rope = banks[(kind, b)]
-            if kind == "V":
-                ot = outs.tile([P, 2, GN], F32, name="ov", tag="ov", bufs=2)
-                for mi in range(2):
-                    nc.scalar.copy(out=ot[:, mi], in_=nope[mi][:])
-                nc.sync.dma_start(out=v_out[b].rearrange("(m p) h d -> p m (h d)", p=P), in_=ot[:])
-                return
+        units = {}
+
+        def out_tile(kind, b):
             ot = outs.tile([P, 2, GH, D_QK], F32, name="ot", tag="ot")
-            for mi in range(2):
-                nc.scalar.copy(out=ot[:, mi, :, :D_NOPE], in_=nope[mi][:].rearrange("p (h d) -> p h d", h=GH))
-            rotate(rope[:], csf, snf, ot[:].rearrange("p m h d -> p (m h) d")[:, :, D_NOPE:])
+            units[(kind, b)] = ot
+
+        def evac_rope(kind, b, add):
+            ot = units[(kind, b)]
+            rotate(banks[(kind, b)][1], add, ot[:].rearrange("p m h d -> p (m h) d")[:, :, D_NOPE:])
+
+        def evac_nope(kind, b, mi, engine_copy):
+            ot = units[(kind, b)]
+            acc = banks[(kind, b)][0][mi]
+            engine_copy(out=ot[:, mi, :, :D_NOPE], in_=acc[:].rearrange("p (h d) -> p h d", h=GH))
+
+        def store(kind, b):
+            ot = units[(kind, b)]
             if kind == "K":
                 dst = k_out[b].rearrange("(m p) h d -> p m (h d)", p=P)
             else:
                 dst = q_out[b].rearrange("(m p) h d -> p m (h d)", p=P)[:, :, kind * GW : (kind + 1) * GW]
             nc.sync.dma_start(out=dst, in_=ot[:].rearrange("p m h d -> p m (h d)"))
 
-        last = {}
+        ve_add = nc.vector.tensor_tensor
 
-        def last_pass(m, g):
-            if g == 0:
-                last[m] = (bank("np", 4), bank("rp" if m % 2 == 0 else "mx", 2))
-            nope, rope = last[m]
-            xm = xflat(m)
-            mm(nope[:], xm, slice(g * P, (g + 1) * P), wcode[(NG - 1, g)], slice(0, GN), g == 0, g == KP - 1)
-            mm(rope[:, :GR], xm, slice(g * P, (g + 1) * P), wcode[(NG - 1, g)], slice(GN, GW), g == 0, g == KP - 1)
+        def burst(kind):
+            for b in range(2):
+                out_tile(kind, b)
+            evac_nope(kind, 0, 0, sc_copy)
+            evac_nope(kind, 0, 1, sc_copy)
+            evac_rope(kind, 0, ve_add)
+            evac_rope(kind, 1, ve_add)
+            evac_nope(kind, 1, 0, sc_copy)
+            evac_nope(kind, 1, 1, sc_copy)
+            store(kind, 0)
+            store(kind, 1)
 
-        def last_evac(m):
-            nope, rope = last[m]
+        def evac_v(b):
+            ov = outs.tile([P, 2, GN], F32, name="ov", tag="ot")
+            for mi in range(2):
+                nc.scalar.copy(out=ov[:, mi], in_=banks[("V", b)][0][mi][:])
+            nc.sync.dma_start(out=v_out[b].rearrange("(m p) h d -> p m (h d)", p=P), in_=ov[:])
+
+        last_out = {}
+
+        def last_rope_mm(b):
+            rope = bank("rp", 2)
+            for mi in range(2):
+                for g in range(KP):
+                    mm(rope[:, mi * GR : (mi + 1) * GR], xflat(2 * b + mi), slice(g * P, (g + 1) * P),
+                       wcode[(NG - 1, g)], slice(GN, GW), g == 0, g == KP - 1)
+            banks[("rope", b)] = rope
+
+        def last_rope(b):
             ot = outs.tile([P, 2, GH, D_QK], F32, name="ot", tag="ot")
-            nc.scalar.copy(out=ot[:, 0, :, :D_NOPE], in_=nope[:].rearrange("p (h d) -> p h d", h=GH))
-            mi = m % 2
-            rotate(rope[:, :GR], csf[:, mi * GR : (mi + 1) * GR], snf[:, mi * GR : (mi + 1) * GR], ot[:, 0, :, D_NOPE:])
-            nc.sync.dma_start(
-                out=q_out[m // 2, mi * P : (mi + 1) * P].rearrange("s h d -> s (h d)")[:, (NG - 1) * GW :],
-                in_=ot[:, 0].rearrange("p h d -> p (h d)"),
+            last_out[b] = ot
+            rotate(banks[("rope", b)], ve_add, ot[:].rearrange("p m h d -> p (m h) d")[:, :, D_NOPE:])
+
+        def last_mm(half, m, g, start, stop):
+            if start:
+                if half == 0:
+                    banks[("lo", m)] = bank("np", 4)
+                else:
+                    banks[("hi", m)] = bank("mx" if m < 2 else "rp", 2)
+            acc = banks[("lo" if half == 0 else "hi", m)]
+            mm(acc[:, :256], xflat(m), slice(g * P, (g + 1) * P), wcode[(NG - 1, g)],
+               slice(half * 256, (half + 1) * 256), start, stop)
+
+        def last_evac(half, m, engine_copy):
+            acc = banks[("lo" if half == 0 else "hi", m)]
+            engine_copy(
+                out=last_out[m // 2][:, m % 2, 2 * half : 2 * half + 2, :D_NOPE],
+                in_=acc[:, :256].rearrange("p (h d) -> p h d", h=2),
             )
 
-        cast_x(0)
-        cast_x(1)
-        turn_x(0)
-        interleave(0)
-        cast_x(2)
-        turn_x(1)
-        quant_x(0)
-        interleave(1)
-        cast_x(3)
-        quant(0)
-        turn_x(2)
-        quant_x(1)
-        interleave(2)
-        quant(1)
-        turn_x(3)
-        quant_x(2)
-        interleave(3)
-        quant(2)
-        quant_x(3)
-        for i in range(4):
-            load(LOOK + i)
+        q4 = q_out.rearrange("b (m p) h d -> p (b m) (h d)", p=P)
 
-        after = {}
-        idx = {key: i for i, key in enumerate(chunks)}
-        after[idx[(0, 1)]] = [lambda: mm_latent(0), lambda: mm_latent(1)]
-        after[idx[(0, 2)]] = [
-            lambda: evac_latent(0), lambda: evac_latent(1), lambda: mm_latent(2), lambda: mm_latent(3), lambda: quant_latent(0)
-        ]
-        after[idx[(0, 3)]] = [lambda: evac_latent(2), lambda: evac_latent(3)]
-        after[idx[("K", 0)]] = [lambda: quant_latent(1), lambda: mm_group(0, 0), lambda: mm_group(0, 1)]
-        after[idx[("V", 0)]] = [lambda: evac(0, 0)]
-        after[idx[(1, 0)]] = [lambda: evac(0, 1), lambda: mm_group("K", 0), lambda: mm_group("K", 1)]
-        after[idx[(1, 1)]] = [lambda: evac("K", 0), lambda: evac("K", 1)]
-        after[idx[(1, 2)]] = [lambda: mm_group("V", 0), lambda: mm_group("V", 1), lambda: evac("V", 0)]
-        after[idx[(1, 3)]] = [lambda: evac("V", 1)]
-        after[idx[(2, 0)]] = [lambda: mm_group(1, 0), lambda: mm_group(1, 1)]
-        after[idx[(2, 1)]] = [lambda: evac(1, 0)]
-        after[idx[(2, 2)]] = [lambda: evac(1, 1)]
-        after[idx[(3, 0)]] = [lambda: mm_group(2, 0), lambda: mm_group(2, 1)]
-        after[idx[(3, 1)]] = [lambda: evac(2, 0)]
-        after[idx[(3, 2)]] = [lambda: evac(2, 1)]
+        def last_store(half, m, n):
+            c0 = (NG - 1) * GW + half * 2 * D_QK
+            nc.sync.dma_start(
+                out=q4[:, m : m + n, c0 : c0 + 2 * D_QK],
+                in_=last_out[m // 2][:, m % 2 : m % 2 + n, 2 * half : 2 * half + 2].rearrange("p m h d -> p m (h d)"),
+            )
 
-        for i in range(4, len(chunks)):
-            load(LOOK + i)
-            interleave(i)
-            quant(i - 1)
-            for f in after.get(i, []):
-                f()
-        for g in range(KP - 1):
-            for m in range(MB):
-                last_pass(m, g)
-        quant(len(chunks) - 1)
         for m in range(MB):
-            last_pass(m, KP - 1)
-            last_evac(m)
+            cast_x(m)
+            turn_x(m)
+            interleave(("L", m))
+        interleave(("K", 0))
+        for m in range(MB):
+            quant_x(m)
+        for g in range(KP):
+            quant(("L", g))
+        interleave(("V", 0))
+        quant(("K", 0))
+        mm_latent(0)
+        mm_latent(1)
+        interleave((0, 0))
+        quant(("V", 0))
+        evac_latent(0)
+        mm_latent(2)
+        evac_latent(1)
+        mm_latent(3)
+        quant_latent(0)
+        interleave((0, 1))
+        quant((0, 0))
+        evac_latent(2)
+        evac_latent(3)
+        mm_group("K", 0)
+        quant((0, 1))
+        quant_latent(1)
+        mm_group("K", 1)
+        interleave((1, 0))
+        load_pair(1, 0)
+        interleave((0, 2))
+        quant((1, 0))
+        load_pair(1, 1)
+        burst("K")
+        mm_group("V", 0)
+        mm_group("V", 1)
+        interleave((0, 3))
+        quant((0, 2))
+        evac_v(0)
+        evac_v(1)
+        quant((0, 3))
+        mm_group(0, 0)
+        mm_group(0, 1)
+        interleave((1, 1))
+        load_pair(1, 2)
+        interleave((1, 2))
+        quant((1, 1))
+        load_pair(1, 3)
+        burst(0)
+        interleave((1, 3))
+        quant((1, 2))
+        interleave((2, 0))
+        quant((1, 3))
+        mm_group(1, 0)
+        mm_group(1, 1)
+        interleave((2, 1))
+        quant((2, 0))
+        interleave((2, 2))
+        quant((2, 1))
+        burst(1)
+        interleave((2, 3))
+        quant((2, 2))
+
+        last_b(0)
+        last_a(0, 0, sc_copy)
+        quant((2, 3))
+        mm_group(2, 0)
+        mm_group(2, 1)
+        last_b(1)
+        last_a(1, 0, sc_copy)
+        last_quant(0, 2)
+        last_b(2)
+        last_quant(1, 2)
+        last_b(3)
+        last_quant(0, 0)
+        last_a(2, 0, sc_copy)
+        last_quant(2, 2)
+        last_quant(3, 2)
+        last_quant(1, 0)
+        burst(2)
+        last_a(3, 0, sc_copy)
+        last_rope_mm(0)
+        last_rope_mm(1)
+        for g in range(2):
+            for m in range(MB):
+                last_mm(0, m, g, g == 0, False)
+        last_quant(2, 0)
+        last_rope(0)
+        last_a(0, 1, sc_copy)
+        last_quant(3, 0)
+        for g in (2, 3):
+            for m in range(MB):
+                last_mm(0, m, g, False, g == 3)
+        last_a(1, 1, sc_copy)
+        last_rope(1)
+        last_quant(0, 1)
+        last_evac(0, 0, sc_copy)
+        last_evac(0, 1, sc_copy)
+        last_store(0, 0, 2)
+        last_quant(1, 1)
+        last_a(2, 1, sc_copy)
+        last_a(3, 1, ve_copy)
+        for g in range(2):
+            for m in range(MB):
+                last_mm(1, m, g, g == 0, False)
+        last_evac(0, 2, ve_copy)
+        last_evac(0, 3, sc_copy)
+        last_store(0, 2, 2)
+        last_quant(3, 1)
+        last_quant(2, 1)
+        for m in range(MB):
+            last_mm(1, m, 3, False, False)
+        for m in range(MB):
+            last_mm(1, m, 2, False, True)
+            last_evac(1, m, sc_copy if m % 2 == 0 else ve_copy)
+            last_store(1, m, 1)

@@ -179,9 +179,14 @@ def tile_multiheadlatentattentionwithgqafused_pa_kernel(
         def weave(engine_copy, dst, src):
             if len(src.shape) == 4:
                 n = src.shape[2]
-                engine_copy(out=dst.rearrange("p (h d j) -> p h d j", h=n, j=4), in_=src.rearrange("p j h d -> p h d j"))
+                engine_copy(
+                    out=dst.rearrange("p (h c i j) -> p h c j i", h=n, i=4, j=4),
+                    in_=src.rearrange("p j h (c i) -> p h c j i", i=4),
+                )
             else:
-                engine_copy(out=dst.rearrange("p (d j) -> p d j", j=4), in_=src.rearrange("p j d -> p d j"))
+                engine_copy(
+                    out=dst.rearrange("p (c i j) -> p c j i", i=4, j=4), in_=src.rearrange("p j (c i) -> p c j i", i=4)
+                )
 
         def interleave(key):
             kind, g = key

import math
from contextlib import ExitStack

import concourse.mybir as mybir
from concourse.masks import make_identity

F32 = mybir.dt.float32
BF16 = mybir.dt.bfloat16
U32 = mybir.dt.uint32
I32 = mybir.dt.int32
U8 = mybir.dt.uint8
E4M3 = mybir.dt.float8_e4m3fn
X4 = mybir.dt.float8_e4m3fn_x4
ALU = mybir.AluOpType
ACT = mybir.ActivationFunctionType

B, S, HID, NH, NKV, LORA, D_ROPE, D_NOPE, D_V = 2, 256, 2048, 16, 4, 512, 64, 128, 128
D_QK = D_NOPE + D_ROPE
P = 128
FLOPS = 2 * B * S * (HID * (NH * D_QK + LORA) + LORA * NKV * (D_QK + D_V))

MB = B * S // P
KP = HID // 512
GH = 4
GW = GH * D_QK
GN = GH * D_NOPE
GR = GH * D_ROPE
NG = NH // GH
HALF = D_ROPE // 2
LATENT_SCALAR = (0, 1, 2)
VECTOR_HEADS = {(0, 0): 4, (2, 0): 4, (0, 3): 2}


def tile_multiheadlatentattentionwithgqafused_pa_kernel(
    tc, x_bytes, x_scale, wqkv, wk_up, wv_up, q_out, k_out, v_out
):
    nc = tc.nc
    with ExitStack() as ctx:
        one = ctx.enter_context(tc.tile_pool(name="one", bufs=1))
        rows = ctx.enter_context(tc.tile_pool(name="rows", bufs=4))
        xpool = ctx.enter_context(tc.tile_pool(name="xpool", bufs=2))
        grp = ctx.enter_context(tc.tile_pool(name="grp", bufs=5))
        codes = ctx.enter_context(tc.tile_pool(name="codes", bufs=9))
        outs = ctx.enter_context(tc.tile_pool(name="outs", bufs=3))
        tmp = ctx.enter_context(tc.tile_pool(name="tmp", bufs=2))
        psum = ctx.enter_context(tc.psum_pool(name="psum", bufs=1))

        def bank(tag, bufs):
            acc = psum.tile([P, 512], F32, name=tag, tag=tag, bufs=bufs)
            return acc

        sc = one.tile([P, KP, 2, 2], F32, name="sc")
        nc.sync.dma_start(
            out=sc[:].rearrange("p g u e -> p g (u e)"),
            in_=x_scale.rearrange("a b (g p t) -> p (a b g) t", p=P, t=4),
        )
        xby = []
        for m in range(MB):
            xb8 = one.tile([P, HID], U8, name="xb8_%d" % m)
            nc.sync.dma_start(out=xb8[:], in_=x_bytes[m // 2, (m % 2) * P : (m % 2 + 1) * P, :])
            xby.append(xb8)

        wq = wqkv.rearrange("(g p j) n -> g p j n", p=P, j=4)
        raw = {}

        def load_small(name, src, tag, bufs):
            w = src.shape[2]
            r = rows.tile([P, 4, w], BF16, name="raw_" + tag, tag=tag, bufs=bufs, align_bytes=64)
            nc.sync.dma_start(out=r[:], in_=src)
            raw[name] = r[:]

        def load_pair(h, g):
            r = rows.tile([P, 4, 2 * GW], BF16, name="raw_q", tag="raw_q", align_bytes=64)
            nc.sync.dma_start(out=r[:], in_=wq[g][:, :, 2 * h * GW : 2 * (h + 1) * GW])
            for i in range(2):
                raw[(2 * h + i, g)] = r[:, :, i * GW : (i + 1) * GW]

        for g in range(KP):
            load_small(("L", g), wq[g][:, :, NH * D_QK :], "raw_l", 4)
        load_small(("K", 0), wk_up.rearrange("(p j) n -> p j n", j=4), "raw_k", 1)
        load_small(("V", 0), wv_up.rearrange("(p j) n -> p j n", j=4), "raw_l", 4)
        for g in range(KP):
            load_pair(0, g)

        pos = one.tile([P, 2], F32, name="pos")
        nc.gpsimd.iota(
            pos[:], pattern=[[P, 2]], base=0, channel_multiplier=1, allow_small_or_imprecise_dtypes=True
        )
        ident = one.tile([P, P], F32, name="ident")
        make_identity(nc, ident[:])
        ang = one.tile([P, 2, 2, HALF], F32, name="ang")
        ratio = 10000.0 ** (-1.0 / HALF)
        nc.vector.tensor_scalar(
            out=ang[:, 0, :, 0:1], in0=pos[:].rearrange("p (m o) -> p m o", o=1), scalar1=1.0, scalar2=None, op0=ALU.mult
        )
        w = 1
        while w < HALF:
            nc.vector.tensor_scalar(
                out=ang[:, 0, :, w : 2 * w], in0=ang[:, 0, :, 0:w], scalar1=ratio**w, scalar2=None, op0=ALU.mult
            )
            w *= 2
        nc.vector.tensor_scalar(
            out=ang[:, 1], in0=ang[:, 0], scalar1=math.pi / 2, scalar2=None, op0=ALU.add
        )
        turn = one.tile([P, 2, 2, HALF], F32, name="turn")
        turn_i = one.tile([P, 2, 2, HALF], I32, name="turn_i")
        nc.vector.tensor_scalar(out=turn[:], in0=ang[:], scalar1=1.0 / (2 * math.pi), scalar2=None, op0=ALU.mult)
        nc.vector.tensor_copy(out=turn_i[:], in_=turn[:])
        nc.vector.tensor_copy(out=turn[:], in_=turn_i[:])
        c1 = 6.28125
        red = one.tile([P, 2, 2, HALF], F32, name="red")
        flat4 = "p a b c -> p (a b c)"
        nc.vector.scalar_tensor_tensor(
            out=red[:].rearrange(flat4), in0=turn[:].rearrange(flat4), scalar=-c1, in1=ang[:].rearrange(flat4),
            op0=ALU.mult, op1=ALU.add,
        )
        red2 = one.tile([P, 2, 2, HALF], F32, name="red2")
        nc.vector.scalar_tensor_tensor(
            out=red2[:].rearrange(flat4), in0=turn[:].rearrange(flat4), scalar=c1 - 2 * math.pi, in1=red[:].rearrange(flat4),
            op0=ALU.mult, op1=ALU.add,
        )
        cs1 = one.tile([P, 2, D_ROPE], F32, name="cs1")
        sn1 = one.tile([P, 2, D_ROPE], F32, name="sn1")
        nc.scalar.activation(out=cs1[:, :, :HALF], in_=red2[:, 1], func=ACT.Sin)
        nc.scalar.activation(out=cs1[:, :, HALF:], in_=red2[:, 1], func=ACT.Sin)
        nc.scalar.activation(out=sn1[:, :, :HALF], in_=red2[:, 0], func=ACT.Sin, scale=-1.0)
        nc.scalar.activation(out=sn1[:, :, HALF:], in_=red2[:, 0], func=ACT.Sin)
        cs = one.tile([P, 2, GH, D_ROPE], F32, name="cs")
        sn = one.tile([P, 2, GH, D_ROPE], F32, name="sn")
        for h in range(GH):
            nc.gpsimd.tensor_scalar(out=cs[:, :, h], in0=cs1[:], scalar1=1.0, scalar2=0.0, op0=ALU.mult, op1=ALU.add)
            nc.gpsimd.tensor_scalar(out=sn[:, :, h], in0=sn1[:], scalar1=1.0, scalar2=0.0, op0=ALU.mult, op1=ALU.add)

        xcast, xgrp, xcode = {}, {}, {}

        def cast_x(m):
            xb = xpool.tile([P, HID], BF16, name="xb", tag="xb", align_bytes=64, bufs=2)
            if m == 0:
                nc.vector.tensor_copy(out=xb[:], in_=xby[m][:].bitcast(E4M3))
            else:
                nc.scalar.copy(out=xb[:], in_=xby[m][:].bitcast(E4M3))
            xcast[m] = xb

        def turn_x(m):
            words = xcast[m][:].bitcast(F32)
            xgf = xpool.tile([P, 2048], BF16, name="xgf", tag="xgf", align_bytes=64, bufs=4)
            xg = xgf[:].rearrange("p (g r u e) -> p g r u e", g=KP, u=2, e=2)
            for half in range(2):
                xt = bank("np", 4)
                for gg in range(2):
                    for u in range(2):
                        g = 2 * half + gg
                        nc.tensor.transpose(
                            xt[:, (2 * gg + u) * P : (2 * gg + u + 1) * P],
                            words[:, 256 * g + u : 256 * (g + 1) : 2],
                            ident[:],
                        )
                halves = xt[:].bitcast(BF16).rearrange("p (g u r e) -> p g r u e", g=2, u=2, e=2)
                for gg in range(2):
                    g = 2 * half + gg
                    nc.vector.tensor_tensor(
                        out=xg[:, g], in0=halves[:, gg], in1=sc[:, g : g + 1].to_broadcast([P, P, 2, 2]), op=ALU.mult
                    )
            xgrp[m] = xgf

        def quant_x(m):
            xc = one.tile([P, KP, P], U32, name="xc_%d" % m, align_bytes=64)
            xs = one.tile([P, KP, P], U8, name="xs_%d" % m, align_bytes=64)
            nc.vector.quantize_mx(
                out=xc[:].rearrange("p g r -> p (g r)").bitcast(X4),
                scales=xs[:].rearrange("p g r -> p (g r)"),
                in_=xgrp[m][:],
            )
            xcode[m] = (xc, xs)

        grouped, wcode = {}, {}
        sc_copy, ve_copy = nc.scalar.copy, nc.vector.tensor_copy

        def weave(engine_copy, dst, src):
            if len(src.shape) == 4:
                n = src.shape[2]
                engine_copy(
                    out=dst.rearrange("p (h c i j) -> p h c j i", h=n, i=4, j=4),
                    in_=src.rearrange("p j h (c i) -> p h c j i", i=4),
                )
            else:
                engine_copy(
                    out=dst.rearrange("p (c i j) -> p c j i", i=4, j=4), in_=src.rearrange("p j (c i) -> p c j i", i=4)
                )

        def interleave(key):
            kind, g = key
            src = raw[key]
            ga = grp.tile([P, 2048], BF16, name="ga", tag="ga", align_bytes=64)
            if kind == "L":
                engine_copy = sc_copy if g in LATENT_SCALAR else ve_copy
                engine_copy(
                    out=ga[:].rearrange("p (t m j) -> p t m j", t=4, j=4),
                    in_=src.rearrange("p j (m t) -> p t m j", t=4),
                )
                grouped[key] = (ga, None)
                return
            if kind == "V":
                weave(sc_copy, ga[:], src)
                grouped[key] = (ga, None)
                return
            heads = src.rearrange("p j (h d) -> p j h d", d=D_QK)
            n = GH - VECTOR_HEADS.get(key, 0)
            if n > 0:
                weave(sc_copy, ga[:, : n * 512], heads[:, :, :n, :D_NOPE])
            if n < GH:
                weave(ve_copy, ga[:, n * 512 :], heads[:, :, n:, :D_NOPE])
            gb = grp.tile([P, 1024], BF16, name="gb", tag="gb", align_bytes=64)
            weave(ve_copy, gb[:], heads[:, :, :, D_NOPE:])
            grouped[key] = (ga, gb)

        def last_a(g, half, engine_copy):
            key = (NG - 1, g)
            ga = last_tiles[g][0]
            heads = raw[key].rearrange("p j (h d) -> p j h d", d=D_QK)
            weave(engine_copy, ga[:, half * 1024 : (half + 1) * 1024], heads[:, :, 2 * half : 2 * half + 2, :D_NOPE])

        def last_b(g):
            key = (NG - 1, g)
            heads = raw[key].rearrange("p j (h d) -> p j h d", d=D_QK)
            ga = grp.tile([P, 2048], BF16, name="ga", tag="ga", align_bytes=64)
            gb = grp.tile([P, 1024], BF16, name="gb", tag="gb", align_bytes=64)
            wc = codes.tile([P, GW], U32, name="wc", tag="wc", align_bytes=64)
            ws = codes.tile([P, GW], U8, name="ws", tag="ws", align_bytes=64)
            last_tiles[g] = (ga, gb)
            wcode[key] = (wc, ws)
            weave(ve_copy, gb[:], heads[:, :, :, D_NOPE:])

        def last_quant(g, part):
            ga, gb = last_tiles[g]
            wc, ws = wcode[(NG - 1, g)]
            cols = slice(part * 256, (part + 1) * 256)
            nc.vector.quantize_mx(
                out=wc[:, cols].bitcast(X4), scales=ws[:, cols],
                in_=gb[:] if part == 2 else ga[:, part * 1024 : (part + 1) * 1024],
            )

        last_tiles = {}

        def quant(key):
            kind = key[0]
            ga, gb = grouped[key]
            if kind in ("L", "K", "V"):
                width = GW if kind == "K" else 512
                wc = one.tile([P, width], U32, name="wc_%s%d" % key, align_bytes=64)
                ws = one.tile([P, width], U8, name="ws_%s%d" % key, align_bytes=64)
            else:
                wc = codes.tile([P, GW], U32, name="wc", tag="wc", align_bytes=64)
                ws = codes.tile([P, GW], U8, name="ws", tag="ws", align_bytes=64)
            nc.vector.quantize_mx(out=wc[:, :512].bitcast(X4), scales=ws[:, :512], in_=ga[:])
            if gb is not None:
                nc.vector.quantize_mx(out=wc[:, 512:].bitcast(X4), scales=ws[:, 512:], in_=gb[:])
            wcode[key] = (wc, ws)

        def mm(out, left, lcols, right, rcols, start, stop):
            nc.tensor.matmul_mx(
                out=out,
                lhsT=left[0][:, lcols].bitcast(X4), lhsT_scale=left[1][:, lcols],
                rhs=right[0][:, rcols].bitcast(X4), rhs_scale=right[1][:, rcols],
                start=start, stop=stop,
            )

        def xflat(m):
            return tuple(t[:].rearrange("p g r -> p (g r)") for t in xcode[m])

        ckg = one.tile([P, MB, P, 4], BF16, name="ckg", align_bytes=64)
        ckc = one.tile([P, MB * P], U32, name="ckc", align_bytes=64)
        cks = one.tile([P, MB * P], U8, name="cks", align_bytes=64)
        ckb = {}

        def mm_latent(m):
            acc = bank("mx", 2)
            for t in range(4):
                for g in range(KP):
                    mm(
                        acc[:, t * P : (t + 1) * P], wcode[("L", g)], slice(t * P, (t + 1) * P),
                        xflat(m), slice(g * P, (g + 1) * P), g == 0, g == KP - 1,
                    )
            ckb[m] = acc

        def evac_latent(m):
            nc.scalar.copy(out=ckg[:, m], in_=ckb[m][:].rearrange("p (t n) -> p n t", t=4))

        def quant_latent(b):
            nc.vector.quantize_mx(
                out=ckc[:, 2 * b * P : 2 * (b + 1) * P].bitcast(X4),
                scales=cks[:, 2 * b * P : 2 * (b + 1) * P],
                in_=ckg[:, 2 * b : 2 * b + 2].rearrange("p m n t -> p (m n t)"),
            )

        banks = {}

        def mm_group(kind, b):
            nope = []
            rope = bank("rp", 2) if kind != "V" else None
            for mi in range(2):
                m = 2 * b + mi
                acc = bank("np", 4)
                if kind in ("K", "V"):
                    mm(acc[:], (ckc, cks), slice(m * P, (m + 1) * P), wcode[(kind, 0)], slice(0, GN), True, True)
                    if kind == "K":
                        mm(rope[:, mi * GR : (mi + 1) * GR], (ckc, cks), slice(m * P, (m + 1) * P),
                           wcode[(kind, 0)], slice(GN, GW), True, True)
                else:
                    for g in range(KP):
                        mm(acc[:], xflat(m), slice(g * P, (g + 1) * P), wcode[(kind, g)], slice(0, GN), g == 0, g == KP - 1)
                    for g in range(KP):
                        mm(rope[:, mi * GR : (mi + 1) * GR], xflat(m), slice(g * P, (g + 1) * P),
                           wcode[(kind, g)], slice(GN, GW), g == 0, g == KP - 1)
                nope.append(acc)
            banks[(kind, b)] = (nope, rope)

        def rotate(rope, add, out):
            a = tmp.tile([P, 512], F32, name="ra", tag="ra")
            c = tmp.tile([P, 512], F32, name="rc", tag="rc")
            nc.vector.tensor_tensor(out=a[:], in0=rope[:], in1=csf, op=ALU.mult)
            four = "p (a s j) -> p a s j"
            nc.vector.tensor_tensor(
                out=c[:].rearrange(four, s=2, j=HALF),
                in0=rope[:].rearrange(four, s=2, j=HALF)[:, :, ::-1, :],
                in1=snf.rearrange(four, s=2, j=HALF),
                op=ALU.mult,
            )
            add(
                out=out,
                in0=a[:].rearrange("p (a d) -> p a d", d=D_ROPE),
                in1=c[:].rearrange("p (a d) -> p a d", d=D_ROPE),
                op=ALU.add,
            )

        csf = cs[:].rearrange("p m h d -> p (m h d)")
        snf = sn[:].rearrange("p m h d -> p (m h d)")

        units = {}

        def out_tile(kind, b):
            ot = outs.tile([P, 2, GH, D_QK], F32, name="ot", tag="ot")
            units[(kind, b)] = ot

        def evac_rope(kind, b, add):
            ot = units[(kind, b)]
            rotate(banks[(kind, b)][1], add, ot[:].rearrange("p m h d -> p (m h) d")[:, :, D_NOPE:])

        def evac_nope(kind, b, mi, engine_copy):
            ot = units[(kind, b)]
            acc = banks[(kind, b)][0][mi]
            engine_copy(out=ot[:, mi, :, :D_NOPE], in_=acc[:].rearrange("p (h d) -> p h d", h=GH))

        def store(kind, b):
            ot = units[(kind, b)]
            if kind == "K":
                dst = k_out[b].rearrange("(m p) h d -> p m (h d)", p=P)
            else:
                dst = q_out[b].rearrange("(m p) h d -> p m (h d)", p=P)[:, :, kind * GW : (kind + 1) * GW]
            nc.sync.dma_start(out=dst, in_=ot[:].rearrange("p m h d -> p m (h d)"))

        ve_add = nc.vector.tensor_tensor

        def burst(kind):
            for b in range(2):
                out_tile(kind, b)
            evac_nope(kind, 0, 0, sc_copy)
            evac_nope(kind, 0, 1, sc_copy)
            evac_rope(kind, 0, ve_add)
            evac_rope(kind, 1, ve_add)
            evac_nope(kind, 1, 0, sc_copy)
            evac_nope(kind, 1, 1, sc_copy)
            store(kind, 0)
            store(kind, 1)

        def evac_v(b):
            ov = outs.tile([P, 2, GN], F32, name="ov", tag="ot")
            for mi in range(2):
                nc.scalar.copy(out=ov[:, mi], in_=banks[("V", b)][0][mi][:])
            nc.sync.dma_start(out=v_out[b].rearrange("(m p) h d -> p m (h d)", p=P), in_=ov[:])

        last_out = {}

        def last_rope_mm(b):
            rope = bank("rp", 2)
            for mi in range(2):
                for g in range(KP):
                    mm(rope[:, mi * GR : (mi + 1) * GR], xflat(2 * b + mi), slice(g * P, (g + 1) * P),
                       wcode[(NG - 1, g)], slice(GN, GW), g == 0, g == KP - 1)
            banks[("rope", b)] = rope

        def last_rope(b):
            ot = outs.tile([P, 2, GH, D_QK], F32, name="ot", tag="ot")
            last_out[b] = ot
            rotate(banks[("rope", b)], ve_add, ot[:].rearrange("p m h d -> p (m h) d")[:, :, D_NOPE:])

        def last_mm(half, m, g, start, stop):
            if start:
                if half == 0:
                    banks[("lo", m)] = bank("np", 4)
                else:
                    banks[("hi", m)] = bank("mx" if m < 2 else "rp", 2)
            acc = banks[("lo" if half == 0 else "hi", m)]
            mm(acc[:, :256], xflat(m), slice(g * P, (g + 1) * P), wcode[(NG - 1, g)],
               slice(half * 256, (half + 1) * 256), start, stop)

        def last_evac(half, m, engine_copy):
            acc = banks[("lo" if half == 0 else "hi", m)]
            engine_copy(
                out=last_out[m // 2][:, m % 2, 2 * half : 2 * half + 2, :D_NOPE],
                in_=acc[:, :256].rearrange("p (h d) -> p h d", h=2),
            )

        q4 = q_out.rearrange("b (m p) h d -> p (b m) (h d)", p=P)

        def last_store(half, m, n):
            c0 = (NG - 1) * GW + half * 2 * D_QK
            nc.sync.dma_start(
                out=q4[:, m : m + n, c0 : c0 + 2 * D_QK],
                in_=last_out[m // 2][:, m % 2 : m % 2 + n, 2 * half : 2 * half + 2].rearrange("p m h d -> p m (h d)"),
            )

        for m in range(MB):
            cast_x(m)
            turn_x(m)
            interleave(("L", m))
        interleave(("K", 0))
        for m in range(MB):
            quant_x(m)
        for g in range(KP):
            quant(("L", g))
        interleave(("V", 0))
        quant(("K", 0))
        mm_latent(0)
        mm_latent(1)
        interleave((0, 0))
        quant(("V", 0))
        evac_latent(0)
        mm_latent(2)
        evac_latent(1)
        mm_latent(3)
        quant_latent(0)
        interleave((0, 1))
        quant((0, 0))
        evac_latent(2)
        evac_latent(3)
        mm_group("K", 0)
        quant((0, 1))
        quant_latent(1)
        mm_group("K", 1)
        interleave((1, 0))
        load_pair(1, 0)
        interleave((0, 2))
        quant((1, 0))
        load_pair(1, 1)
        burst("K")
        mm_group("V", 0)
        mm_group("V", 1)
        interleave((0, 3))
        quant((0, 2))
        evac_v(0)
        evac_v(1)
        quant((0, 3))
        mm_group(0, 0)
        mm_group(0, 1)
        interleave((1, 1))
        load_pair(1, 2)
        interleave((1, 2))
        quant((1, 1))
        load_pair(1, 3)
        burst(0)
        interleave((1, 3))
        quant((1, 2))
        interleave((2, 0))
        quant((1, 3))
        mm_group(1, 0)
        mm_group(1, 1)
        interleave((2, 1))
        quant((2, 0))
        interleave((2, 2))
        quant((2, 1))
        burst(1)
        interleave((2, 3))
        quant((2, 2))

        last_b(0)
        last_a(0, 0, sc_copy)
        quant((2, 3))
        mm_group(2, 0)
        mm_group(2, 1)
        last_b(1)
        last_a(1, 0, sc_copy)
        last_quant(0, 2)
        last_b(2)
        last_quant(1, 2)
        last_b(3)
        last_quant(0, 0)
        last_a(2, 0, sc_copy)
        last_quant(2, 2)
        last_quant(3, 2)
        last_quant(1, 0)
        burst(2)
        last_a(3, 0, sc_copy)
        last_rope_mm(0)
        last_rope_mm(1)
        for g in range(2):
            for m in range(MB):
                last_mm(0, m, g, g == 0, False)
        last_quant(2, 0)
        last_rope(0)
        last_a(0, 1, sc_copy)
        last_quant(3, 0)
        for g in (2, 3):
            for m in range(MB):
                last_mm(0, m, g, False, g == 3)
        last_a(1, 1, sc_copy)
        last_rope(1)
        last_quant(0, 1)
        last_evac(0, 0, sc_copy)
        last_evac(0, 1, sc_copy)
        last_store(0, 0, 2)
        last_quant(1, 1)
        last_a(2, 1, sc_copy)
        last_a(3, 1, ve_copy)
        for g in range(2):
            for m in range(MB):
                last_mm(1, m, g, g == 0, False)
        last_evac(0, 2, ve_copy)
        last_evac(0, 3, sc_copy)
        last_store(0, 2, 2)
        last_quant(3, 1)
        last_quant(2, 1)
        for m in range(MB):
            last_mm(1, m, 3, False, False)
        for m in range(MB):
            last_mm(1, m, 2, False, True)
            last_evac(1, m, sc_copy if m % 2 == 0 else ve_copy)
            last_store(1, m, 1)
